import numpy as np
import ml_dtypes


def mxq(x, axis, fmt="e4m3"):
    dtype, down = {"e4m3": (ml_dtypes.float8_e4m3fn, 7), "e5m2": (ml_dtypes.float8_e5m2, 14)}[fmt]
    v = np.moveaxis(np.asarray(x, np.float32).astype(ml_dtypes.bfloat16).astype(np.float64), axis, -1)
    blocks = v.reshape(v.shape[:-1] + (-1, 32))
    amax = np.abs(blocks).max(-1, keepdims=True)
    byte = np.maximum(np.where(amax > 0, np.frexp(amax)[1] - 1 + 127, 0) - down, 1)
    scale = np.exp2(byte - 127.0)
    codes = (blocks / scale).astype(np.float32).astype(dtype).astype(np.float64)
    return np.moveaxis((codes * scale).reshape(v.shape), -1, axis)


WIDE = False


def mx_kscale(k):
    if not WIDE:
        return np.ones(k)
    levels = np.array([10, -10, 5, -5, 0])
    if k % 512:
        return np.exp2(np.random.permutation(np.resize(levels, k // 32))).repeat(32)
    a = np.empty((k // 512, 16))
    for p in range(k // 512):
        a[p, :8] = np.random.permutation(np.resize(levels, 8))
        for g in range(8):
            far = levels[np.abs(levels - a[p, g]) >= 10]
            a[p, g + 8] = far[np.random.randint(len(far))]
    return np.exp2(a.ravel()).repeat(32)


BF16 = ml_dtypes.bfloat16


def bf(x):
    return np.asarray(x, np.float32).astype(BF16)


def f64(x):
    return np.asarray(x).astype(np.float64)


B, IN_F, OUT_F = 4096, 2048, 512
IN_Q = IN_F // 4
OUT_Q = OUT_F // 4


def setup_inputs():
    s = mx_kscale(IN_Q)
    scale = 1.0 / np.sqrt(IN_Q)
    inp = {"x": bf((np.random.standard_normal((B, 4, IN_Q)) * s).reshape(B, IN_F))}
    for name in ["rr", "ri", "rj", "rk"]:
        inp["W_" + name] = bf(np.random.uniform(-scale, scale, (OUT_Q, IN_Q)) / s[None, :])
    for name in ["rr", "ri", "rj", "rk"]:
        inp["b_" + name] = bf(np.random.standard_normal(OUT_Q) * 0.5)
    return inp


def reference(x, W_rr, W_ri, W_rj, W_rk, b_rr, b_ri, b_rj, b_rk):
    b = x.shape[0]
    xs = f64(x).reshape(b, 4, IN_Q)
    W = np.stack([f64(W_rr), f64(W_ri), f64(W_rj), f64(W_rk)])
    bias = np.stack([f64(b_rr), f64(b_ri), f64(b_rj), f64(b_rk)])
    xq = mxq(xs, 2, "e4m3")
    Wq = mxq(W, 2, "e4m3")
    Y = (xq.reshape(b * 4, IN_Q) @ Wq.reshape(4 * OUT_Q, IN_Q).T).reshape(b, 4, 4, OUT_Q) + bias
    out_r = Y[:, 0, 0] - Y[:, 1, 1] - Y[:, 2, 2] - Y[:, 3, 3]
    out_i = Y[:, 0, 1] + Y[:, 1, 0] + Y[:, 2, 3] - Y[:, 3, 2]
    out_j = Y[:, 0, 2] - Y[:, 1, 3] + Y[:, 2, 0] + Y[:, 3, 1]
    out_k = Y[:, 0, 3] + Y[:, 1, 2] - Y[:, 2, 1] + Y[:, 3, 0]
    out = np.stack([out_r, out_i, out_j, out_k], axis=1)
    return out.reshape(b, -1)

@@ -1,0 +1,210 @@
+from contextlib import ExitStack
+
+import concourse.mybir as mybir
+from concourse.masks import make_identity
+
+F32 = mybir.dt.float32
+BF16 = mybir.dt.bfloat16
+U32 = mybir.dt.uint32
+U8 = mybir.dt.uint8
+I32 = mybir.dt.int32
+FP8X4 = mybir.dt.float8_e4m3fn_x4
+ADD = mybir.AluOpType.add
+MULT = mybir.AluOpType.mult
+
+P = 128
+TILES = 32
+FLOPS = 2 * 16384 * 512 * 512
+
+GROUPS = [[2 * g, 2 * g + 1] for g in range(16)]
+LOADS = [(0, 1), (1, 1)] + [(2 * g, 2) for g in range(1, 16)]
+LOADS_AHEAD = 9
+
+
+def tile_qdense_t_kernel(tc, x, W_rr, W_ri, W_rj, W_rk, b_rr, b_ri, b_rj, b_rk, out):
+    nc = tc.nc
+    weights = [W_rr, W_ri, W_rj, W_rk]
+    biases = [b_rr, b_ri, b_rj, b_rk]
+    x_rows = x.rearrange("(p t) k -> p t k", t=TILES)
+    out_rows = out.rearrange("(p t) n -> p t n", t=TILES)
+
+    with ExitStack() as ctx:
+        const = ctx.enter_context(tc.tile_pool(name="const", bufs=1))
+        xpool = ctx.enter_context(tc.tile_pool(name="xres", bufs=1))
+        gpool = ctx.enter_context(tc.tile_pool(name="grouped", bufs=4))
+        qpool = ctx.enter_context(tc.tile_pool(name="codes", bufs=8))
+        opool = ctx.enter_context(tc.tile_pool(name="outs", bufs=6))
+        psum = ctx.enter_context(tc.psum_pool(name="psum", bufs=1))
+        ctx.enter_context(tc.manual_schedule())
+
+        banks_used = [0]
+
+        def new_bank():
+            b = banks_used[0] % 8
+            banks_used[0] += 1
+            return psum.tile([P, 512], F32, name="bank%d" % b, tag="bank%d" % b)
+
+        ident = const.tile([P, P], F32, name="ident")
+        make_identity(nc, ident[:])
+        q_scales = const.tile([P, 1024], U8, name="q_scales", align_bytes=64)
+        nc.vector.memset(q_scales[:].bitcast(I32), 0)
+        b_rows = const.tile([P, P], BF16, name="b_rows")
+        nc.vector.memset(b_rows[:], 0.0)
+        ones = const.tile([P, P], BF16, name="ones")
+        nc.vector.memset(ones[:], 1.0)
+        signs = const.tile([P, 4, P], BF16, name="signs")
+        nc.vector.memset(signs[:], 1.0)
+        nc.vector.memset(signs[32:64, 0, :], -1.0)
+        nc.vector.memset(signs[64:128, 0, :], -1.0)
+        nc.vector.memset(signs[64:96, 1, :], -1.0)
+        nc.vector.memset(signs[96:128, 2, :], -1.0)
+        nc.vector.memset(signs[32:64, 3, :], -1.0)
+
+        w_sb = const.tile([P, 2048], BF16, name="w_sb")
+        for q in range(4):
+            nc.sync.dma_start(out=w_sb[:, 512 * q:512 * (q + 1)], in_=weights[q])
+        for q in range(4):
+            nc.scalar.dma_start(out=b_rows[32 * q:32 * q + 1, :],
+                                in_=biases[q].rearrange("(o n) -> o n", o=1))
+
+        x_words = {}
+
+        def load(i):
+            t0, nt = LOADS[i]
+            xs = xpool.tile([P, nt * 2048], BF16, name="x%d" % t0)
+            nc.sync.dma_start(out=xs[:].rearrange("p (t k) -> p t k", t=nt),
+                              in_=x_rows[:, t0:t0 + nt, :])
+            words = xs[:].bitcast(F32)
+            for j in range(nt):
+                x_words[t0 + j] = words[:, 1024 * j:1024 * (j + 1)]
+
+        for i in range(LOADS_AHEAD):
+            load(i)
+
+        def flip(words):
+            got = []
+            for h in range(2):
+                bank = new_bank()
+                for s in range(4):
+                    nc.tensor.transpose(bank[:, P * s:P * (s + 1)],
+                                        words[:, 512 * h + 256 * (s // 2) + s % 2:512 * h + 256 * (s // 2 + 1):2],
+                                        ident[:])
+                got.append(bank)
+            return got
+
+        def regroup(engine_copy, bank, dst_words):
+            engine_copy(out=dst_words.rearrange("p (c r u) -> p c r u", c=2, u=2),
+                        in_=bank[:].rearrange("p (c u r) -> p c r u", c=2, u=2))
+
+        w_banks = flip(w_sb[:].bitcast(F32))
+        w_pn = const.tile([P, 4096], BF16, name="w_pn", align_bytes=64)
+        w_pn_words = w_pn[:].bitcast(F32)
+        regroup(nc.scalar.copy, w_banks[0], w_pn_words[:, 0:512])
+
+        b_signed = const.tile([P, 4, P], BF16, name="b_signed")
+        nc.vector.tensor_tensor(out=b_signed[:], in0=signs[:],
+                                in1=b_rows[:].unsqueeze(1).to_broadcast([P, 4, P]), op=MULT)
+        regroup(nc.vector.tensor_copy, w_banks[1], w_pn_words[:, 512:1024])
+
+        bias_ps = new_bank()
+        nc.tensor.matmul(bias_ps[:], lhsT=ones[:], rhs=b_signed[:].rearrange("p o n -> p (o n)"),
+                         start=True, stop=True)
+        bias_bc = const.tile([P, 512], F32, name="bias_bc")
+        nc.scalar.copy(out=bias_bc[:], in_=bias_ps[:])
+
+        q_codes = const.tile([P, 1024], U32, name="q_codes", align_bytes=64)
+        nc.vector.quantize_mx(out=q_codes[:, 0:512].bitcast(FP8X4), scales=q_scales[:, 0:512],
+                              in_=w_pn[:, 0:2048])
+        pos = w_pn[:, 0:2048].rearrange("p (q e) -> p q e", q=4)
+        neg = w_pn[:, 2048:4096].rearrange("p (q e) -> p q e", q=4)
+        nc.vector.tensor_scalar_mul(out=neg[:, 0:2, :], in0=pos[:, 1:4:2, :], scalar1=-1.0)
+        nc.vector.tensor_scalar_mul(out=neg[:, 2:4, :], in0=pos[:, 2:4, :], scalar1=-1.0)
+        nc.vector.quantize_mx(out=q_codes[:, 512:1024].bitcast(FP8X4), scales=q_scales[:, 512:1024],
+                              in_=w_pn[:, 2048:4096])
+
+        r_codes = const.tile([P, 1536], U32, name="r_codes", align_bytes=64)
+        r_scales = const.tile([P, 1536], U8, name="r_scales", align_bytes=64)
+        views = [
+            (r_codes[:].bitcast(I32).rearrange("p (d w) -> p d w", d=12),
+             q_codes[:].bitcast(I32).rearrange("p (d w) -> p d w", d=8)),
+            (r_scales[:].bitcast(I32).rearrange("p (d w) -> p d w", d=12),
+             q_scales[:].bitcast(I32).rearrange("p (d w) -> p d w", d=8)),
+        ]
+
+        def move(dst, src):
+            for r_v, q_v in views:
+                nc.vector.tensor_copy(out=r_v[:, dst, :], in_=q_v[:, src, :])
+
+        rhs = [(q_codes[:, 0:512], q_scales[:, 0:512])]
+        for c in range(3):
+            rhs.append((r_codes[:, 512 * c:512 * (c + 1)], r_scales[:, 512 * c:512 * (c + 1)]))
+
+        t_banks = {}
+        grouped = {}
+        packed = {}
+
+        def stage_t(g):
+            for t in GROUPS[g]:
+                t_banks[t] = flip(x_words[t])
+
+        def stage_c(g):
+            for t in GROUPS[g]:
+                gr = gpool.tile([P, 2048], BF16, name="grouped", tag="grouped", align_bytes=64)
+                gw = gr[:].bitcast(F32)
+                for h in range(2):
+                    regroup(nc.scalar.copy, t_banks[t][h], gw[:, 512 * h:512 * (h + 1)])
+                grouped[t] = gr
+
+        def stage_q(t):
+            codes = qpool.tile([P, 512], U32, name="codes", tag="codes", align_bytes=64)
+            scales = qpool.tile([P, 512], U8, name="scales", tag="scales", align_bytes=64)
+            nc.vector.quantize_mx(out=codes[:].bitcast(FP8X4), scales=scales[:], in_=grouped[t][:])
+            packed[t] = (codes, scales)
+
+        accs = {}
+
+        def stage_m(g):
+            for t in GROUPS[g]:
+                acc = new_bank()
+                codes, scales = packed[t]
+                for c in range(4):
+                    nc.tensor.matmul_mx(out=acc[:],
+                                        lhsT=codes[:, P * c:P * (c + 1)].bitcast(FP8X4),
+                                        lhsT_scale=scales[:, P * c:P * (c + 1)],
+                                        rhs=rhs[c][0].bitcast(FP8X4),
+                                        rhs_scale=rhs[c][1],
+                                        start=(c == 0), stop=(c == 3))
+                accs[t] = acc
+
+        stage_t(0)
+        stage_c(0)
+        move(slice(0, 5, 2), slice(4, 7))
+        move(slice(1, 4, 2), slice(0, 3, 2))
+        stage_q(GROUPS[0][0])
+        move(slice(7, 10), slice(4, 7))
+        move(slice(6, 11, 4), slice(0, 2))
+        move(slice(5, 6), slice(3, 4))
+        move(slice(11, 12), slice(0, 1))
+        stage_q(GROUPS[0][1])
+
+        next_load = LOADS_AHEAD
+        n_groups = len(GROUPS)
+        for g in range(n_groups):
+            last = g == n_groups - 1
+            if not last:
+                stage_t(g + 1)
+                stage_c(g + 1)
+            stage_m(g)
+            tiles = GROUPS[g]
+            ot = opool.tile([P, len(tiles), 512], F32, name="ot", tag="ot")
+            for j, t in enumerate(tiles):
+                if not last:
+                    stage_q(GROUPS[g + 1][j])
+                nc.vector.tensor_tensor(out=ot[:, j, :], in0=accs[t][:], in1=bias_bc[:], op=ADD)
+                if last:
+                    nc.sync.dma_start(out=out_rows[:, t:t + 1, :], in_=ot[:, j:j + 1, :])
+            if not last:
+                nc.sync.dma_start(out=out_rows[:, tiles[0]:tiles[0] + len(tiles), :], in_=ot[:])
+            if next_load < len(LOADS):
+                load(next_load)
+                next_load += 1

@@ -16,9 +16,22 @@ P = 128
 TILES = 32
 FLOPS = 2 * 16384 * 512 * 512
 
-GROUPS = [[2 * g, 2 * g + 1] for g in range(16)]
-LOADS = [(0, 1), (1, 1)] + [(2 * g, 2) for g in range(1, 16)]
+T_BANKS = 6
+M_BANKS = 2
+STRIDED = 4
+T_RUNS = [4, 2] + [4] * 6 + [2]
+M_RUNS = [2, 2, 2] + [4] * 6 + [2]
+LOADS = [(0, 1), (1, 1)] + [(2 * i, 2) for i in range(1, 16)]
 LOADS_AHEAD = 9
+
+
+def cut(runs):
+    got = []
+    first = 0
+    for n in runs:
+        got.append(list(range(first, first + n)))
+        first += n
+    return got
 
 
 def tile_qdense_t_kernel(tc, x, W_rr, W_ri, W_rj, W_rk, b_rr, b_ri, b_rj, b_rk, out):
@@ -30,35 +43,28 @@ def tile_qdense_t_kernel(tc, x, W_rr, W_ri, W_rj, W_rk, b_rr, b_ri, b_rj, b_rk, 
 
     with ExitStack() as ctx:
         const = ctx.enter_context(tc.tile_pool(name="const", bufs=1))
-        xpool = ctx.enter_context(tc.tile_pool(name="xres", bufs=1))
-        gpool = ctx.enter_context(tc.tile_pool(name="grouped", bufs=4))
-        qpool = ctx.enter_context(tc.tile_pool(name="codes", bufs=8))
-        opool = ctx.enter_context(tc.tile_pool(name="outs", bufs=6))
+        xpool = ctx.enter_context(tc.tile_pool(name="xin", bufs=9))
+        ppool = ctx.enter_context(tc.tile_pool(name="sorted", bufs=6))
+        gpool = ctx.enter_context(tc.tile_pool(name="grouped", bufs=5))
+        qpool = ctx.enter_context(tc.tile_pool(name="codes", bufs=10))
+        opool = ctx.enter_context(tc.tile_pool(name="outs", bufs=5))
         psum = ctx.enter_context(tc.psum_pool(name="psum", bufs=1))
         ctx.enter_context(tc.manual_schedule())
 
-        banks_used = [0]
+        used = {"t": 0, "m": 0}
 
-        def new_bank():
-            b = banks_used[0] % 8
-            banks_used[0] += 1
-            return psum.tile([P, 512], F32, name="bank%d" % b, tag="bank%d" % b)
+        def new_bank(kind):
+            b = used[kind] % (T_BANKS if kind == "t" else M_BANKS)
+            used[kind] += 1
+            return psum.tile([P, 512], F32, name="%s%d" % (kind, b), tag="%s%d" % (kind, b))
 
         ident = const.tile([P, P], F32, name="ident")
         make_identity(nc, ident[:])
-        q_scales = const.tile([P, 1024], U8, name="q_scales", align_bytes=64)
-        nc.vector.memset(q_scales[:].bitcast(I32), 0)
+        warm = const.tile([P, 1], F32, name="warm")
+        nc.vector.memset(warm[:], 0.0)
         b_rows = const.tile([P, P], BF16, name="b_rows")
         nc.vector.memset(b_rows[:], 0.0)
-        ones = const.tile([P, P], BF16, name="ones")
-        nc.vector.memset(ones[:], 1.0)
-        signs = const.tile([P, 4, P], BF16, name="signs")
-        nc.vector.memset(signs[:], 1.0)
-        nc.vector.memset(signs[32:64, 0, :], -1.0)
-        nc.vector.memset(signs[64:128, 0, :], -1.0)
-        nc.vector.memset(signs[64:96, 1, :], -1.0)
-        nc.vector.memset(signs[96:128, 2, :], -1.0)
-        nc.vector.memset(signs[32:64, 3, :], -1.0)
+        nc.scalar.copy(out=warm[:], in_=warm[:])
 
         w_sb = const.tile([P, 2048], BF16, name="w_sb")
         for q in range(4):
@@ -71,8 +77,8 @@ def tile_qdense_t_kernel(tc, x, W_rr, W_ri, W_rj, W_rk, b_rr, b_ri, b_rj, b_rk, 
 
         def load(i):
             t0, nt = LOADS[i]
-            xs = xpool.tile([P, nt * 2048], BF16, name="x%d" % t0)
-            nc.sync.dma_start(out=xs[:].rearrange("p (t k) -> p t k", t=nt),
+            xs = xpool.tile([P, 4096], BF16, name="x", tag="x")
+            nc.sync.dma_start(out=xs[:, 0:2048 * nt].rearrange("p (t k) -> p t k", t=nt),
                               in_=x_rows[:, t0:t0 + nt, :])
             words = xs[:].bitcast(F32)
             for j in range(nt):
@@ -81,36 +87,75 @@ def tile_qdense_t_kernel(tc, x, W_rr, W_ri, W_rj, W_rk, b_rr, b_ri, b_rj, b_rk, 
         for i in range(LOADS_AHEAD):
             load(i)
 
-        def flip(words):
-            got = []
-            for h in range(2):
-                bank = new_bank()
-                for s in range(4):
-                    nc.tensor.transpose(bank[:, P * s:P * (s + 1)],
-                                        words[:, 512 * h + 256 * (s // 2) + s % 2:512 * h + 256 * (s // 2 + 1):2],
-                                        ident[:])
-                got.append(bank)
-            return got
+        q_scales = const.tile([P, 1024], U8, name="q_scales", align_bytes=64)
+        nc.vector.memset(q_scales[:].bitcast(I32), 0)
+        ones = const.tile([P, P], BF16, name="ones")
+        nc.vector.memset(ones[:], 1.0)
+        signs = const.tile([P, 4, P], BF16, name="signs")
+        nc.vector.memset(signs[:], 1.0)
+        nc.vector.memset(signs[32:64, 0, :], -1.0)
+        nc.vector.memset(signs[64:128, 0, :], -1.0)
+        nc.vector.memset(signs[64:96, 1, :], -1.0)
+        nc.vector.memset(signs[96:128, 2, :], -1.0)
+        nc.vector.memset(signs[32:64, 3, :], -1.0)
+
+        def flip(words, h, is_sorted):
+            bank = new_bank("t")
+            for c in range(2):
+                for u in range(2):
+                    base = 512 * h + 256 * c
+                    if is_sorted:
+                        cols = words[:, base + P * u:base + P * (u + 1)]
+                    else:
+                        cols = words[:, base + u:base + 256:2]
+                    s = 2 * c + u
+                    nc.tensor.transpose(bank[:, P * s:P * (s + 1)], cols, ident[:])
+            return bank
 
         def regroup(engine_copy, bank, dst_words):
             engine_copy(out=dst_words.rearrange("p (c r u) -> p c r u", c=2, u=2),
                         in_=bank[:].rearrange("p (c u r) -> p c r u", c=2, u=2))
 
-        w_banks = flip(w_sb[:].bitcast(F32))
+        grouped = {}
+        packed = {}
+        accs = {}
+        done_words = {}
+        outs = {}
+
+        def put_in_order(t, engine_copy):
+            ps = ppool.tile([P, 1024], F32, name="sorted", tag="sorted", align_bytes=64)
+            engine_copy(out=ps[:].rearrange("p (c u r) -> p c u r", c=4, u=2),
+                        in_=x_words[t].rearrange("p (c r u) -> p c u r", c=4, u=2))
+            done_words[t] = ps[:]
+
+        def turn(t):
+            gr = gpool.tile([P, 2048], BF16, name="grouped", tag="grouped", align_bytes=64)
+            gw = gr[:].bitcast(F32)
+            for h in range(2):
+                if t in done_words:
+                    bank = flip(done_words[t], h, True)
+                else:
+                    bank = flip(x_words[t], h, False)
+                regroup(nc.scalar.copy, bank, gw[:, 512 * h:512 * (h + 1)])
+            grouped[t] = gr
+
+        def quantise(t):
+            codes = qpool.tile([P, 512], U32, name="codes", tag="codes", align_bytes=64)
+            scales = qpool.tile([P, 512], U8, name="scales", tag="scales", align_bytes=64)
+            nc.vector.quantize_mx(out=codes[:].bitcast(FP8X4), scales=scales[:], in_=grouped[t][:])
+            packed[t] = (codes, scales)
+
         w_pn = const.tile([P, 4096], BF16, name="w_pn", align_bytes=64)
         w_pn_words = w_pn[:].bitcast(F32)
+        w_words = w_sb[:].bitcast(F32)
+        w_banks = [flip(w_words, 0, False), flip(w_words, 1, False)]
         regroup(nc.scalar.copy, w_banks[0], w_pn_words[:, 0:512])
-
-        b_signed = const.tile([P, 4, P], BF16, name="b_signed")
-        nc.vector.tensor_tensor(out=b_signed[:], in0=signs[:],
-                                in1=b_rows[:].unsqueeze(1).to_broadcast([P, 4, P]), op=MULT)
         regroup(nc.vector.tensor_copy, w_banks[1], w_pn_words[:, 512:1024])
 
-        bias_ps = new_bank()
-        nc.tensor.matmul(bias_ps[:], lhsT=ones[:], rhs=b_signed[:].rearrange("p o n -> p (o n)"),
-                         start=True, stop=True)
-        bias_bc = const.tile([P, 512], F32, name="bias_bc")
-        nc.scalar.copy(out=bias_bc[:], in_=bias_ps[:])
+        t_runs = cut(T_RUNS)
+        m_runs = cut(M_RUNS)
+        for t in t_runs[0]:
+            turn(t)
 
         q_codes = const.tile([P, 1024], U32, name="q_codes", align_bytes=64)
         nc.vector.quantize_mx(out=q_codes[:, 0:512].bitcast(FP8X4), scales=q_scales[:, 0:512],
@@ -119,6 +164,7 @@ def tile_qdense_t_kernel(tc, x, W_rr, W_ri, W_rj, W_rk, b_rr, b_ri, b_rj, b_rk, 
         neg = w_pn[:, 2048:4096].rearrange("p (q e) -> p q e", q=4)
         nc.vector.tensor_scalar_mul(out=neg[:, 0:2, :], in0=pos[:, 1:4:2, :], scalar1=-1.0)
         nc.vector.tensor_scalar_mul(out=neg[:, 2:4, :], in0=pos[:, 2:4, :], scalar1=-1.0)
+        quantise(0)
         nc.vector.quantize_mx(out=q_codes[:, 512:1024].bitcast(FP8X4), scales=q_scales[:, 512:1024],
                               in_=w_pn[:, 2048:4096])
 
@@ -139,72 +185,79 @@ def tile_qdense_t_kernel(tc, x, W_rr, W_ri, W_rj, W_rk, b_rr, b_ri, b_rj, b_rk, 
         for c in range(3):
             rhs.append((r_codes[:, 512 * c:512 * (c + 1)], r_scales[:, 512 * c:512 * (c + 1)]))
 
-        t_banks = {}
-        grouped = {}
-        packed = {}
-
-        def stage_t(g):
-            for t in GROUPS[g]:
-                t_banks[t] = flip(x_words[t])
-
-        def stage_c(g):
-            for t in GROUPS[g]:
-                gr = gpool.tile([P, 2048], BF16, name="grouped", tag="grouped", align_bytes=64)
-                gw = gr[:].bitcast(F32)
-                for h in range(2):
-                    regroup(nc.scalar.copy, t_banks[t][h], gw[:, 512 * h:512 * (h + 1)])
-                grouped[t] = gr
-
-        def stage_q(t):
-            codes = qpool.tile([P, 512], U32, name="codes", tag="codes", align_bytes=64)
-            scales = qpool.tile([P, 512], U8, name="scales", tag="scales", align_bytes=64)
-            nc.vector.quantize_mx(out=codes[:].bitcast(FP8X4), scales=scales[:], in_=grouped[t][:])
-            packed[t] = (codes, scales)
-
-        accs = {}
-
-        def stage_m(g):
-            for t in GROUPS[g]:
-                acc = new_bank()
-                codes, scales = packed[t]
-                for c in range(4):
-                    nc.tensor.matmul_mx(out=acc[:],
-                                        lhsT=codes[:, P * c:P * (c + 1)].bitcast(FP8X4),
-                                        lhsT_scale=scales[:, P * c:P * (c + 1)],
-                                        rhs=rhs[c][0].bitcast(FP8X4),
-                                        rhs_scale=rhs[c][1],
-                                        start=(c == 0), stop=(c == 3))
-                accs[t] = acc
-
-        stage_t(0)
-        stage_c(0)
-        move(slice(0, 5, 2), slice(4, 7))
         move(slice(1, 4, 2), slice(0, 3, 2))
-        stage_q(GROUPS[0][0])
-        move(slice(7, 10), slice(4, 7))
         move(slice(6, 11, 4), slice(0, 2))
         move(slice(5, 6), slice(3, 4))
         move(slice(11, 12), slice(0, 1))
-        stage_q(GROUPS[0][1])
+        move(slice(0, 5, 2), slice(4, 7))
+        move(slice(7, 10), slice(4, 7))
+        quantise(1)
 
-        next_load = LOADS_AHEAD
-        n_groups = len(GROUPS)
-        for g in range(n_groups):
-            last = g == n_groups - 1
-            if not last:
-                stage_t(g + 1)
-                stage_c(g + 1)
-            stage_m(g)
-            tiles = GROUPS[g]
-            ot = opool.tile([P, len(tiles), 512], F32, name="ot", tag="ot")
-            for j, t in enumerate(tiles):
-                if not last:
-                    stage_q(GROUPS[g + 1][j])
-                nc.vector.tensor_tensor(out=ot[:, j, :], in0=accs[t][:], in1=bias_bc[:], op=ADD)
-                if last:
-                    nc.sync.dma_start(out=out_rows[:, t:t + 1, :], in_=ot[:, j:j + 1, :])
-            if not last:
-                nc.sync.dma_start(out=out_rows[:, tiles[0]:tiles[0] + len(tiles), :], in_=ot[:])
-            if next_load < len(LOADS):
-                load(next_load)
-                next_load += 1
+        b_signed = const.tile([P, 4, P], BF16, name="b_signed")
+        nc.vector.tensor_tensor(out=b_signed[:], in0=signs[:],
+                                in1=b_rows[:].unsqueeze(1).to_broadcast([P, 4, P]), op=MULT)
+
+        def multiply(t):
+            acc = new_bank("m")
+            codes, scales = packed[t]
+            for c in range(4):
+                nc.tensor.matmul_mx(out=acc[:],
+                                    lhsT=codes[:, P * c:P * (c + 1)].bitcast(FP8X4),
+                                    lhsT_scale=scales[:, P * c:P * (c + 1)],
+                                    rhs=rhs[c][0].bitcast(FP8X4),
+                                    rhs_scale=rhs[c][1],
+                                    start=(c == 0), stop=(c == 3))
+            accs[t] = acc
+
+        bias_bc = const.tile([P, 512], F32, name="bias_bc")
+        next_load = [LOADS_AHEAD]
+
+        def finish(t):
+            if t % 2 == 0:
+                outs[t // 2] = opool.tile([P, 2, 512], F32, name="ot", tag="ot")
+            ot = outs[t // 2]
+            nc.vector.tensor_tensor(out=ot[:, t % 2, :], in0=accs[t][:], in1=bias_bc[:], op=ADD)
+            if t >= TILES - 2:
+                nc.sync.dma_start(out=out_rows[:, t:t + 1, :], in_=ot[:, t % 2:t % 2 + 1, :])
+            elif t % 2 == 1:
+                nc.sync.dma_start(out=out_rows[:, t - 1:t + 1, :], in_=ot[:])
+                if next_load[0] < len(LOADS):
+                    load(next_load[0])
+                    next_load[0] += 1
+
+        carried = []
+        for k in range(len(m_runs)):
+            if k == 0:
+                turns = []
+                to_quantise = t_runs[0][2:]
+            else:
+                turns = t_runs[k] if k < len(t_runs) else []
+                to_quantise = list(turns)
+            for t in turns:
+                turn(t)
+            for t in carried:
+                finish(t)
+            carried = []
+            ahead = t_runs[k + 1] if k + 1 < len(t_runs) else []
+            for t in ahead:
+                if t % 4 == 3:
+                    put_in_order(t, nc.scalar.copy)
+                else:
+                    put_in_order(t, nc.vector.tensor_copy)
+            if k == 0:
+                bias_ps = new_bank("t")
+                nc.tensor.matmul(bias_ps[:], lhsT=ones[:], rhs=b_signed[:].rearrange("p o n -> p (o n)"),
+                                 start=True, stop=True)
+                nc.scalar.copy(out=bias_bc[:], in_=bias_ps[:])
+            runs = m_runs[k]
+            for j, t in enumerate(runs):
+                multiply(t)
+                lo = j * len(to_quantise) // len(runs)
+                hi = (j + 1) * len(to_quantise) // len(runs)
+                for tq in to_quantise[lo:hi]:
+                    quantise(tq)
+                if j >= 1:
+                    finish(runs[j - 1])
+            carried = [runs[-1]]
+        for t in carried:
+            finish(t)

@@ -16,13 +16,12 @@ P = 128
 TILES = 32
 FLOPS = 2 * 16384 * 512 * 512
 
-T_BANKS = 6
-M_BANKS = 2
-STRIDED = 4
-T_RUNS = [4, 2] + [4] * 6 + [2]
+T_BANKS = 5
+M_BANKS = 3
+T_RUNS = [2] + [4] * 7 + [2]
 M_RUNS = [2, 2, 2] + [4] * 6 + [2]
 LOADS = [(0, 1), (1, 1)] + [(2 * i, 2) for i in range(1, 16)]
-LOADS_AHEAD = 9
+LOADS_AHEAD = 11
 
 
 def cut(runs):
@@ -43,11 +42,11 @@ def tile_qdense_t_kernel(tc, x, W_rr, W_ri, W_rj, W_rk, b_rr, b_ri, b_rj, b_rk, 
 
     with ExitStack() as ctx:
         const = ctx.enter_context(tc.tile_pool(name="const", bufs=1))
-        xpool = ctx.enter_context(tc.tile_pool(name="xin", bufs=9))
+        xpool = ctx.enter_context(tc.tile_pool(name="xin", bufs=10))
         ppool = ctx.enter_context(tc.tile_pool(name="sorted", bufs=6))
         gpool = ctx.enter_context(tc.tile_pool(name="grouped", bufs=5))
         qpool = ctx.enter_context(tc.tile_pool(name="codes", bufs=10))
-        opool = ctx.enter_context(tc.tile_pool(name="outs", bufs=5))
+        opool = ctx.enter_context(tc.tile_pool(name="outs", bufs=6))
         psum = ctx.enter_context(tc.psum_pool(name="psum", bufs=1))
         ctx.enter_context(tc.manual_schedule())
 
@@ -77,8 +76,11 @@ def tile_qdense_t_kernel(tc, x, W_rr, W_ri, W_rj, W_rk, b_rr, b_ri, b_rj, b_rk, 
 
         def load(i):
             t0, nt = LOADS[i]
-            xs = xpool.tile([P, 4096], BF16, name="x", tag="x")
-            nc.sync.dma_start(out=xs[:, 0:2048 * nt].rearrange("p (t k) -> p t k", t=nt),
+            if nt == 1:
+                xs = const.tile([P, 2048], BF16, name="x%d" % t0)
+            else:
+                xs = xpool.tile([P, 2048 * nt], BF16, name="x", tag="x")
+            nc.sync.dma_start(out=xs[:].rearrange("p (t k) -> p t k", t=nt),
                               in_=x_rows[:, t0:t0 + nt, :])
             words = xs[:].bitcast(F32)
             for j in range(nt):
@@ -98,6 +100,9 @@ def tile_qdense_t_kernel(tc, x, W_rr, W_ri, W_rj, W_rk, b_rr, b_ri, b_rj, b_rk, 
         nc.vector.memset(signs[64:96, 1, :], -1.0)
         nc.vector.memset(signs[96:128, 2, :], -1.0)
         nc.vector.memset(signs[32:64, 3, :], -1.0)
+        b_signed = const.tile([P, 4, P], BF16, name="b_signed")
+        nc.gpsimd.tensor_tensor(out=b_signed[:], in0=signs[:],
+                                in1=b_rows[:].unsqueeze(1).to_broadcast([P, 4, P]), op=MULT)
 
         def flip(words, h, is_sorted):
             bank = new_bank("t")
@@ -122,7 +127,8 @@ def tile_qdense_t_kernel(tc, x, W_rr, W_ri, W_rj, W_rk, b_rr, b_ri, b_rj, b_rk, 
         done_words = {}
         outs = {}
 
-        def put_in_order(t, engine_copy):
+        def put_in_order(t):
+            engine_copy = nc.scalar.copy if t % 4 == 3 else nc.vector.tensor_copy
             ps = ppool.tile([P, 1024], F32, name="sorted", tag="sorted", align_bytes=64)
             engine_copy(out=ps[:].rearrange("p (c u r) -> p c u r", c=4, u=2),
                         in_=x_words[t].rearrange("p (c r u) -> p c u r", c=4, u=2))
@@ -157,29 +163,27 @@ def tile_qdense_t_kernel(tc, x, W_rr, W_ri, W_rj, W_rk, b_rr, b_ri, b_rj, b_rk, 
         for t in t_runs[0]:
             turn(t)
 
-        q_codes = const.tile([P, 1024], U32, name="q_codes", align_bytes=64)
-        nc.vector.quantize_mx(out=q_codes[:, 0:512].bitcast(FP8X4), scales=q_scales[:, 0:512],
-                              in_=w_pn[:, 0:2048])
         pos = w_pn[:, 0:2048].rearrange("p (q e) -> p q e", q=4)
         neg = w_pn[:, 2048:4096].rearrange("p (q e) -> p q e", q=4)
         nc.vector.tensor_scalar_mul(out=neg[:, 0:2, :], in0=pos[:, 1:4:2, :], scalar1=-1.0)
         nc.vector.tensor_scalar_mul(out=neg[:, 2:4, :], in0=pos[:, 2:4, :], scalar1=-1.0)
-        quantise(0)
+        q_codes = const.tile([P, 1024], U32, name="q_codes", align_bytes=64)
+        nc.vector.quantize_mx(out=q_codes[:, 0:512].bitcast(FP8X4), scales=q_scales[:, 0:512],
+                              in_=w_pn[:, 0:2048])
         nc.vector.quantize_mx(out=q_codes[:, 512:1024].bitcast(FP8X4), scales=q_scales[:, 512:1024],
                               in_=w_pn[:, 2048:4096])
+        quantise(0)
 
         r_codes = const.tile([P, 1536], U32, name="r_codes", align_bytes=64)
         r_scales = const.tile([P, 1536], U8, name="r_scales", align_bytes=64)
-        views = [
-            (r_codes[:].bitcast(I32).rearrange("p (d w) -> p d w", d=12),
-             q_codes[:].bitcast(I32).rearrange("p (d w) -> p d w", d=8)),
-            (r_scales[:].bitcast(I32).rearrange("p (d w) -> p d w", d=12),
-             q_scales[:].bitcast(I32).rearrange("p (d w) -> p d w", d=8)),
-        ]
+        r_code_blocks = r_codes[:].bitcast(I32).rearrange("p (d w) -> p d w", d=12)
+        q_code_blocks = q_codes[:].bitcast(I32).rearrange("p (d w) -> p d w", d=8)
+        r_scale_blocks = r_scales[:].bitcast(I32).rearrange("p (d w) -> p d w", d=12)
+        q_scale_blocks = q_scales[:].bitcast(I32).rearrange("p (d w) -> p d w", d=8)
 
         def move(dst, src):
-            for r_v, q_v in views:
-                nc.vector.tensor_copy(out=r_v[:, dst, :], in_=q_v[:, src, :])
+            nc.vector.tensor_copy(out=r_code_blocks[:, dst, :], in_=q_code_blocks[:, src, :])
+            nc.gpsimd.tensor_copy(out=r_scale_blocks[:, dst, :], in_=q_scale_blocks[:, src, :])
 
         rhs = [(q_codes[:, 0:512], q_scales[:, 0:512])]
         for c in range(3):
@@ -193,9 +197,11 @@ def tile_qdense_t_kernel(tc, x, W_rr, W_ri, W_rj, W_rk, b_rr, b_ri, b_rj, b_rk, 
         move(slice(7, 10), slice(4, 7))
         quantise(1)
 
-        b_signed = const.tile([P, 4, P], BF16, name="b_signed")
-        nc.vector.tensor_tensor(out=b_signed[:], in0=signs[:],
-                                in1=b_rows[:].unsqueeze(1).to_broadcast([P, 4, P]), op=MULT)
+        bias_ps = new_bank("t")
+        nc.tensor.matmul(bias_ps[:], lhsT=ones[:], rhs=b_signed[:].rearrange("p o n -> p (o n)"),
+                         start=True, stop=True)
+        bias_bc = const.tile([P, 512], F32, name="bias_bc")
+        nc.scalar.copy(out=bias_bc[:], in_=bias_ps[:])
 
         def multiply(t):
             acc = new_bank("m")
@@ -209,7 +215,6 @@ def tile_qdense_t_kernel(tc, x, W_rr, W_ri, W_rj, W_rk, b_rr, b_ri, b_rj, b_rk, 
                                     start=(c == 0), stop=(c == 3))
             accs[t] = acc
 
-        bias_bc = const.tile([P, 512], F32, name="bias_bc")
         next_load = [LOADS_AHEAD]
 
         def finish(t):
@@ -227,37 +232,32 @@ def tile_qdense_t_kernel(tc, x, W_rr, W_ri, W_rj, W_rk, b_rr, b_ri, b_rj, b_rk, 
 
         carried = []
         for k in range(len(m_runs)):
-            if k == 0:
-                turns = []
-                to_quantise = t_runs[0][2:]
-            else:
-                turns = t_runs[k] if k < len(t_runs) else []
-                to_quantise = list(turns)
+            turns = t_runs[k] if 0 < k < len(t_runs) else []
             for t in turns:
                 turn(t)
             for t in carried:
                 finish(t)
-            carried = []
             ahead = t_runs[k + 1] if k + 1 < len(t_runs) else []
-            for t in ahead:
-                if t % 4 == 3:
-                    put_in_order(t, nc.scalar.copy)
-                else:
-                    put_in_order(t, nc.vector.tensor_copy)
-            if k == 0:
-                bias_ps = new_bank("t")
-                nc.tensor.matmul(bias_ps[:], lhsT=ones[:], rhs=b_signed[:].rearrange("p o n -> p (o n)"),
-                                 start=True, stop=True)
-                nc.scalar.copy(out=bias_bc[:], in_=bias_ps[:])
             runs = m_runs[k]
+            n_sorted = 0 if k < 2 else 4
+            for t in ahead[0:n_sorted]:
+                put_in_order(t)
+            share = -(-(len(ahead) - n_sorted) // max(1, len(runs) - 0))
+            n_quantised = 0
             for j, t in enumerate(runs):
+                while t not in packed:
+                    quantise(turns[n_quantised])
+                    n_quantised += 1
                 multiply(t)
-                lo = j * len(to_quantise) // len(runs)
-                hi = (j + 1) * len(to_quantise) // len(runs)
-                for tq in to_quantise[lo:hi]:
+                for tq in turns[n_quantised:n_quantised + -(-len(turns) // len(runs))]:
                     quantise(tq)
+                    n_quantised += 1
                 if j >= 1:
                     finish(runs[j - 1])
+                if j >= 0:
+                    for ta in ahead[n_sorted:n_sorted + share]:
+                        put_in_order(ta)
+                        n_sorted += 1
             carried = [runs[-1]]
         for t in carried:
             finish(t)

@@ -18,8 +18,7 @@ FLOPS = 2 * 16384 * 512 * 512
 
 T_BANKS = 5
 M_BANKS = 3
-T_RUNS = [2] + [4] * 7 + [2]
-M_RUNS = [2, 2, 2] + [4] * 6 + [2]
+RUNS = [2] * 16
 LOADS = [(0, 1), (1, 1)] + [(2 * i, 2) for i in range(1, 16)]
 LOADS_AHEAD = 11
 
@@ -158,9 +157,8 @@ def tile_qdense_t_kernel(tc, x, W_rr, W_ri, W_rj, W_rk, b_rr, b_ri, b_rj, b_rk, 
         regroup(nc.scalar.copy, w_banks[0], w_pn_words[:, 0:512])
         regroup(nc.vector.tensor_copy, w_banks[1], w_pn_words[:, 512:1024])
 
-        t_runs = cut(T_RUNS)
-        m_runs = cut(M_RUNS)
-        for t in t_runs[0]:
+        runs = cut(RUNS)
+        for t in runs[0]:
             turn(t)
 
         pos = w_pn[:, 0:2048].rearrange("p (q e) -> p q e", q=4)
@@ -197,6 +195,8 @@ def tile_qdense_t_kernel(tc, x, W_rr, W_ri, W_rj, W_rk, b_rr, b_ri, b_rj, b_rk, 
         move(slice(7, 10), slice(4, 7))
         quantise(1)
 
+        for t in runs[2]:
+            put_in_order(t)
         bias_ps = new_bank("t")
         nc.tensor.matmul(bias_ps[:], lhsT=ones[:], rhs=b_signed[:].rearrange("p o n -> p (o n)"),
                          start=True, stop=True)
@@ -231,33 +231,27 @@ def tile_qdense_t_kernel(tc, x, W_rr, W_ri, W_rj, W_rk, b_rr, b_ri, b_rj, b_rk, 
                     next_load[0] += 1
 
         carried = []
-        for k in range(len(m_runs)):
-            turns = t_runs[k] if 0 < k < len(t_runs) else []
+        for k in range(len(runs)):
+            turns = runs[k + 1] if k + 1 < len(runs) else []
             for t in turns:
                 turn(t)
             for t in carried:
                 finish(t)
-            ahead = t_runs[k + 1] if k + 1 < len(t_runs) else []
-            runs = m_runs[k]
-            n_sorted = 0 if k < 2 else 4
-            for t in ahead[0:n_sorted]:
-                put_in_order(t)
-            share = -(-(len(ahead) - n_sorted) // max(1, len(runs) - 0))
-            n_quantised = 0
-            for j, t in enumerate(runs):
-                while t not in packed:
-                    quantise(turns[n_quantised])
-                    n_quantised += 1
+            ahead = runs[k + 3] if k + 3 < len(runs) else []
+            for n, t in enumerate(runs[k]):
                 multiply(t)
-                for tq in turns[n_quantised:n_quantised + -(-len(turns) // len(runs))]:
-                    quantise(tq)
-                    n_quantised += 1
-                if j >= 1:
-                    finish(runs[j - 1])
-                if j >= 0:
-                    for ta in ahead[n_sorted:n_sorted + share]:
+                if n == 0:
+                    for ta in ahead[0:1]:
                         put_in_order(ta)
-                        n_sorted += 1
-            carried = [runs[-1]]
+                if n < len(turns):
+                    quantise(turns[n])
+                if n >= 1:
+                    finish(runs[k][n - 1])
+                if n == len(runs[k]) - 1:
+                    for tq in turns[len(runs[k]):]:
+                        quantise(tq)
+                    for ta in ahead[1:]:
+                        put_in_order(ta)
+            carried = [runs[k][-1]]
         for t in carried:
             finish(t)

@@ -99,9 +99,6 @@ def tile_qdense_t_kernel(tc, x, W_rr, W_ri, W_rj, W_rk, b_rr, b_ri, b_rj, b_rk, 
         nc.vector.memset(signs[64:96, 1, :], -1.0)
         nc.vector.memset(signs[96:128, 2, :], -1.0)
         nc.vector.memset(signs[32:64, 3, :], -1.0)
-        b_signed = const.tile([P, 4, P], BF16, name="b_signed")
-        nc.gpsimd.tensor_tensor(out=b_signed[:], in0=signs[:],
-                                in1=b_rows[:].unsqueeze(1).to_broadcast([P, 4, P]), op=MULT)
 
         def flip(words, h, is_sorted):
             bank = new_bank("t")
@@ -181,7 +178,7 @@ def tile_qdense_t_kernel(tc, x, W_rr, W_ri, W_rj, W_rk, b_rr, b_ri, b_rj, b_rk, 
 
         def move(dst, src):
             nc.vector.tensor_copy(out=r_code_blocks[:, dst, :], in_=q_code_blocks[:, src, :])
-            nc.gpsimd.tensor_copy(out=r_scale_blocks[:, dst, :], in_=q_scale_blocks[:, src, :])
+            nc.vector.tensor_copy(out=r_scale_blocks[:, dst, :], in_=q_scale_blocks[:, src, :])
 
         rhs = [(q_codes[:, 0:512], q_scales[:, 0:512])]
         for c in range(3):
@@ -193,15 +190,20 @@ def tile_qdense_t_kernel(tc, x, W_rr, W_ri, W_rj, W_rk, b_rr, b_ri, b_rj, b_rk, 
         move(slice(11, 12), slice(0, 1))
         move(slice(0, 5, 2), slice(4, 7))
         move(slice(7, 10), slice(4, 7))
+        b_signed = const.tile([P, 4, P], BF16, name="b_signed")
+        nc.vector.tensor_tensor(out=b_signed[:], in0=signs[:],
+                                in1=b_rows[:].unsqueeze(1).to_broadcast([P, 4, P]), op=MULT)
         quantise(1)
 
         for t in runs[2]:
             put_in_order(t)
-        bias_ps = new_bank("t")
-        nc.tensor.matmul(bias_ps[:], lhsT=ones[:], rhs=b_signed[:].rearrange("p o n -> p (o n)"),
-                         start=True, stop=True)
         bias_bc = const.tile([P, 512], F32, name="bias_bc")
-        nc.scalar.copy(out=bias_bc[:], in_=bias_ps[:])
+
+        def spread_bias():
+            bias_ps = new_bank("t")
+            nc.tensor.matmul(bias_ps[:], lhsT=ones[:], rhs=b_signed[:].rearrange("p o n -> p (o n)"),
+                             start=True, stop=True)
+            nc.scalar.copy(out=bias_bc[:], in_=bias_ps[:])
 
         def multiply(t):
             acc = new_bank("m")
@@ -235,6 +237,8 @@ def tile_qdense_t_kernel(tc, x, W_rr, W_ri, W_rj, W_rk, b_rr, b_ri, b_rj, b_rk, 
             turns = runs[k + 1] if k + 1 < len(runs) else []
             for t in turns:
                 turn(t)
+            if k == 0:
+                spread_bias()
             for t in carried:
                 finish(t)
             ahead = runs[k + 3] if k + 3 < len(runs) else []

@@ -19,8 +19,8 @@ FLOPS = 2 * 16384 * 512 * 512
 T_BANKS = 5
 M_BANKS = 3
 RUNS = [2] * 16
-LOADS = [(0, 1), (1, 1)] + [(2 * i, 2) for i in range(1, 16)]
-LOADS_AHEAD = 11
+LOADS = [(t, 1) for t in range(4)] + [(2 * i, 2) for i in range(2, 16)]
+LOADS_AHEAD = 13
 
 
 def cut(runs):
@@ -41,7 +41,7 @@ def tile_qdense_t_kernel(tc, x, W_rr, W_ri, W_rj, W_rk, b_rr, b_ri, b_rj, b_rk, 
 
     with ExitStack() as ctx:
         const = ctx.enter_context(tc.tile_pool(name="const", bufs=1))
-        xpool = ctx.enter_context(tc.tile_pool(name="xin", bufs=10))
+        xpool = ctx.enter_context(tc.tile_pool(name="xin", bufs=9))
         ppool = ctx.enter_context(tc.tile_pool(name="sorted", bufs=6))
         gpool = ctx.enter_context(tc.tile_pool(name="grouped", bufs=5))
         qpool = ctx.enter_context(tc.tile_pool(name="codes", bufs=10))
@@ -206,16 +206,21 @@ def tile_qdense_t_kernel(tc, x, W_rr, W_ri, W_rj, W_rk, b_rr, b_ri, b_rj, b_rk, 
             nc.scalar.copy(out=bias_bc[:], in_=bias_ps[:])
 
         def multiply(t):
-            acc = new_bank("m")
             codes, scales = packed[t]
-            for c in range(4):
-                nc.tensor.matmul_mx(out=acc[:],
-                                    lhsT=codes[:, P * c:P * (c + 1)].bitcast(FP8X4),
-                                    lhsT_scale=scales[:, P * c:P * (c + 1)],
-                                    rhs=rhs[c][0].bitcast(FP8X4),
-                                    rhs_scale=rhs[c][1],
-                                    start=(c == 0), stop=(c == 3))
-            accs[t] = acc
+            parts = 2 if t == TILES - 1 else 1
+            width = 512 // parts
+            accs[t] = []
+            for part in range(parts):
+                acc = new_bank("m")
+                cols = slice(width * part, width * (part + 1))
+                for c in range(4):
+                    nc.tensor.matmul_mx(out=acc[:, 0:width],
+                                        lhsT=codes[:, P * c:P * (c + 1)].bitcast(FP8X4),
+                                        lhsT_scale=scales[:, P * c:P * (c + 1)],
+                                        rhs=rhs[c][0][:, cols].bitcast(FP8X4),
+                                        rhs_scale=rhs[c][1][:, cols],
+                                        start=(c == 0), stop=(c == 3))
+                accs[t].append((acc, width, cols))
 
         next_load = [LOADS_AHEAD]
 
@@ -223,10 +228,11 @@ def tile_qdense_t_kernel(tc, x, W_rr, W_ri, W_rj, W_rk, b_rr, b_ri, b_rj, b_rk, 
             if t % 2 == 0:
                 outs[t // 2] = opool.tile([P, 2, 512], F32, name="ot", tag="ot")
             ot = outs[t // 2]
-            nc.vector.tensor_tensor(out=ot[:, t % 2, :], in0=accs[t][:], in1=bias_bc[:], op=ADD)
-            if t >= TILES - 2:
-                nc.sync.dma_start(out=out_rows[:, t:t + 1, :], in_=ot[:, t % 2:t % 2 + 1, :])
-            elif t % 2 == 1:
+            for acc, width, cols in accs[t]:
+                nc.vector.tensor_tensor(out=ot[:, t % 2, cols], in0=acc[:, 0:width], in1=bias_bc[:, cols], op=ADD)
+                if t >= TILES - 2:
+                    nc.sync.dma_start(out=out_rows[:, t, cols], in_=ot[:, t % 2, cols])
+            if t % 2 == 1 and t < TILES - 2:
                 nc.sync.dma_start(out=out_rows[:, t - 1:t + 1, :], in_=ot[:])
                 if next_load[0] < len(LOADS):
                     load(next_load[0])
@@ -237,13 +243,13 @@ def tile_qdense_t_kernel(tc, x, W_rr, W_ri, W_rj, W_rk, b_rr, b_ri, b_rj, b_rk, 
             turns = runs[k + 1] if k + 1 < len(runs) else []
             for t in turns:
                 turn(t)
-            if k == 0:
-                spread_bias()
             for t in carried:
                 finish(t)
             ahead = runs[k + 3] if k + 3 < len(runs) else []
             for n, t in enumerate(runs[k]):
                 multiply(t)
+                if t == runs[0][-1]:
+                    spread_bias()
                 if n == 0:
                     for ta in ahead[0:1]:
                         put_in_order(ta)

@@ -67,10 +67,6 @@ def tile_qdense_t_kernel(tc, x, W_rr, W_ri, W_rj, W_rk, b_rr, b_ri, b_rj, b_rk, 
         w_sb = const.tile([P, 2048], BF16, name="w_sb")
         for q in range(4):
             nc.sync.dma_start(out=w_sb[:, 512 * q:512 * (q + 1)], in_=weights[q])
-        for q in range(4):
-            nc.scalar.dma_start(out=b_rows[32 * q:32 * q + 1, :],
-                                in_=biases[q].rearrange("(o n) -> o n", o=1))
-
         x_words = {}
 
         def load(i):
@@ -85,7 +81,12 @@ def tile_qdense_t_kernel(tc, x, W_rr, W_ri, W_rj, W_rk, b_rr, b_ri, b_rj, b_rk, 
             for j in range(nt):
                 x_words[t0 + j] = words[:, 1024 * j:1024 * (j + 1)]
 
-        for i in range(LOADS_AHEAD):
+        for i in range(4):
+            load(i)
+        for q in range(4):
+            nc.scalar.dma_start(out=b_rows[32 * q:32 * q + 1, :],
+                                in_=biases[q].rearrange("(o n) -> o n", o=1))
+        for i in range(4, LOADS_AHEAD):
             load(i)
 
         q_scales = const.tile([P, 1024], U8, name="q_scales", align_bytes=64)
@@ -190,10 +191,10 @@ def tile_qdense_t_kernel(tc, x, W_rr, W_ri, W_rj, W_rk, b_rr, b_ri, b_rj, b_rk, 
         move(slice(11, 12), slice(0, 1))
         move(slice(0, 5, 2), slice(4, 7))
         move(slice(7, 10), slice(4, 7))
+        quantise(1)
         b_signed = const.tile([P, 4, P], BF16, name="b_signed")
         nc.vector.tensor_tensor(out=b_signed[:], in0=signs[:],
                                 in1=b_rows[:].unsqueeze(1).to_broadcast([P, 4, P]), op=MULT)
-        quantise(1)
 
         for t in runs[2]:
             put_in_order(t)

@@ -16,11 +16,12 @@ P = 128
 TILES = 32
 FLOPS = 2 * 16384 * 512 * 512
 
-T_BANKS = 5
-M_BANKS = 3
+T_BANKS = 4
+M_BANKS = 4
 RUNS = [2] * 16
-LOADS = [(t, 1) for t in range(4)] + [(2 * i, 2) for i in range(2, 16)]
-LOADS_AHEAD = 13
+LOADS = [(t, 1) for t in range(4)] + [(t, 2) for t in range(4, 12, 2)] + [(t, 4) for t in range(12, 32, 4)]
+LOADS_AHEAD = 11
+STORE_TILES = 4
 
 
 def cut(runs):
@@ -41,11 +42,11 @@ def tile_qdense_t_kernel(tc, x, W_rr, W_ri, W_rj, W_rk, b_rr, b_ri, b_rj, b_rk, 
 
     with ExitStack() as ctx:
         const = ctx.enter_context(tc.tile_pool(name="const", bufs=1))
-        xpool = ctx.enter_context(tc.tile_pool(name="xin", bufs=9))
+        xpool = ctx.enter_context(tc.tile_pool(name="xin", bufs=3))
         ppool = ctx.enter_context(tc.tile_pool(name="sorted", bufs=6))
         gpool = ctx.enter_context(tc.tile_pool(name="grouped", bufs=5))
         qpool = ctx.enter_context(tc.tile_pool(name="codes", bufs=10))
-        opool = ctx.enter_context(tc.tile_pool(name="outs", bufs=6))
+        opool = ctx.enter_context(tc.tile_pool(name="outs", bufs=4))
         psum = ctx.enter_context(tc.psum_pool(name="psum", bufs=1))
         ctx.enter_context(tc.manual_schedule())
 
@@ -71,8 +72,8 @@ def tile_qdense_t_kernel(tc, x, W_rr, W_ri, W_rj, W_rk, b_rr, b_ri, b_rj, b_rk, 
 
         def load(i):
             t0, nt = LOADS[i]
-            if nt == 1:
-                xs = const.tile([P, 2048], BF16, name="x%d" % t0)
+            if t0 < 12:
+                xs = const.tile([P, 2048 * nt], BF16, name="x%d" % t0)
             else:
                 xs = xpool.tile([P, 2048 * nt], BF16, name="x", tag="x")
             nc.sync.dma_start(out=xs[:].rearrange("p (t k) -> p t k", t=nt),
@@ -177,18 +178,20 @@ def tile_qdense_t_kernel(tc, x, W_rr, W_ri, W_rj, W_rk, b_rr, b_ri, b_rj, b_rk, 
         r_scale_blocks = r_scales[:].bitcast(I32).rearrange("p (d w) -> p d w", d=12)
         q_scale_blocks = q_scales[:].bitcast(I32).rearrange("p (d w) -> p d w", d=8)
 
-        def move(dst, src):
-            nc.vector.tensor_copy(out=r_code_blocks[:, dst, :], in_=q_code_blocks[:, src, :])
-            nc.vector.tensor_copy(out=r_scale_blocks[:, dst, :], in_=q_scale_blocks[:, src, :])
+        def move(dst, src, repeat=1):
+            for r_blocks, q_blocks, words in [(r_code_blocks, q_code_blocks, P), (r_scale_blocks, q_scale_blocks, P // 4)]:
+                blocks = q_blocks[:, src, :]
+                if repeat > 1:
+                    blocks = blocks.to_broadcast([P, repeat, words])
+                nc.vector.tensor_copy(out=r_blocks[:, dst, :], in_=blocks)
 
         rhs = [(q_codes[:, 0:512], q_scales[:, 0:512])]
         for c in range(3):
             rhs.append((r_codes[:, 512 * c:512 * (c + 1)], r_scales[:, 512 * c:512 * (c + 1)]))
 
-        move(slice(1, 4, 2), slice(0, 3, 2))
-        move(slice(6, 11, 4), slice(0, 2))
-        move(slice(5, 6), slice(3, 4))
-        move(slice(11, 12), slice(0, 1))
+        move(slice(1, 12, 5), slice(0, 1), repeat=3)
+        move(slice(3, 6, 2), slice(2, 4))
+        move(slice(10, 11), slice(1, 2))
         move(slice(0, 5, 2), slice(4, 7))
         move(slice(7, 10), slice(4, 7))
         quantise(1)
@@ -201,7 +204,7 @@ def tile_qdense_t_kernel(tc, x, W_rr, W_ri, W_rj, W_rk, b_rr, b_ri, b_rj, b_rk, 
         bias_bc = const.tile([P, 512], F32, name="bias_bc")
 
         def spread_bias():
-            bias_ps = new_bank("t")
+            bias_ps = new_bank("m")
             nc.tensor.matmul(bias_ps[:], lhsT=ones[:], rhs=b_signed[:].rearrange("p o n -> p (o n)"),
                              start=True, stop=True)
             nc.scalar.copy(out=bias_bc[:], in_=bias_ps[:])
@@ -223,22 +226,21 @@ def tile_qdense_t_kernel(tc, x, W_rr, W_ri, W_rj, W_rk, b_rr, b_ri, b_rj, b_rk, 
                                         start=(c == 0), stop=(c == 3))
                 accs[t].append((acc, width, cols))
 
-        next_load = [LOADS_AHEAD]
-
         def finish(t):
-            if t % 2 == 0:
-                outs[t // 2] = opool.tile([P, 2, 512], F32, name="ot", tag="ot")
-            ot = outs[t // 2]
+            j = t % STORE_TILES
+            if j == 0:
+                outs[t // STORE_TILES] = opool.tile([P, STORE_TILES, 512], F32, name="ot", tag="ot")
+            ot = outs[t // STORE_TILES]
             for acc, width, cols in accs[t]:
-                nc.vector.tensor_tensor(out=ot[:, t % 2, cols], in0=acc[:, 0:width], in1=bias_bc[:, cols], op=ADD)
+                nc.vector.tensor_tensor(out=ot[:, j, cols], in0=acc[:, 0:width], in1=bias_bc[:, cols], op=ADD)
                 if t >= TILES - 2:
-                    nc.sync.dma_start(out=out_rows[:, t, cols], in_=ot[:, t % 2, cols])
-            if t % 2 == 1 and t < TILES - 2:
-                nc.sync.dma_start(out=out_rows[:, t - 1:t + 1, :], in_=ot[:])
-                if next_load[0] < len(LOADS):
-                    load(next_load[0])
-                    next_load[0] += 1
+                    nc.sync.dma_start(out=out_rows[:, t, cols], in_=ot[:, j, cols])
+            if t == TILES - 3:
+                nc.sync.dma_start(out=out_rows[:, t - 1:t + 1, :], in_=ot[:, 0:2, :])
+            elif j == STORE_TILES - 1 and t < TILES - 2:
+                nc.sync.dma_start(out=out_rows[:, t - j:t + 1, :], in_=ot[:])
 
+        n_loaded = LOADS_AHEAD
         carried = []
         for k in range(len(runs)):
             turns = runs[k + 1] if k + 1 < len(runs) else []
@@ -247,13 +249,15 @@ def tile_qdense_t_kernel(tc, x, W_rr, W_ri, W_rj, W_rk, b_rr, b_ri, b_rj, b_rk, 
             for t in carried:
                 finish(t)
             ahead = runs[k + 3] if k + 3 < len(runs) else []
+            n_sorted = 0
             for n, t in enumerate(runs[k]):
                 multiply(t)
                 if t == runs[0][-1]:
                     spread_bias()
-                if n == 0:
+                if n == 0 and k >= 3:
                     for ta in ahead[0:1]:
                         put_in_order(ta)
+                        n_sorted += 1
                 if n < len(turns):
                     quantise(turns[n])
                 if n >= 1:
@@ -261,8 +265,11 @@ def tile_qdense_t_kernel(tc, x, W_rr, W_ri, W_rj, W_rk, b_rr, b_ri, b_rj, b_rk, 
                 if n == len(runs[k]) - 1:
                     for tq in turns[len(runs[k]):]:
                         quantise(tq)
-                    for ta in ahead[1:]:
+                    for ta in ahead[n_sorted:]:
                         put_in_order(ta)
+            if n_loaded < len(LOADS) and LOADS[n_loaded][0] - 12 + 4 <= runs[k][-1] + 7:
+                load(n_loaded)
+                n_loaded += 1
             carried = [runs[k][-1]]
         for t in carried:
             finish(t)

@@ -61,6 +61,14 @@ def tile_qdense_t_kernel(tc, x, W_rr, W_ri, W_rj, W_rk, b_rr, b_ri, b_rj, b_rk, 
         make_identity(nc, ident[:])
         warm = const.tile([P, 1], F32, name="warm")
         nc.vector.memset(warm[:], 0.0)
+        filler = const.tile([P, 512], BF16, name="filler")
+        nc.vector.memset(filler[:], 0.0)
+        filler_ps = new_bank("m")
+
+        def keep_busy(n):
+            for i in range(n):
+                nc.tensor.matmul(filler_ps[:], lhsT=filler[:, 0:P], rhs=filler[:], start=True, stop=True)
+
         b_rows = const.tile([P, P], BF16, name="b_rows")
         nc.vector.memset(b_rows[:], 0.0)
         nc.scalar.copy(out=warm[:], in_=warm[:])
@@ -152,13 +160,16 @@ def tile_qdense_t_kernel(tc, x, W_rr, W_ri, W_rj, W_rk, b_rr, b_ri, b_rj, b_rk, 
         w_pn = const.tile([P, 4096], BF16, name="w_pn", align_bytes=64)
         w_pn_words = w_pn[:].bitcast(F32)
         w_words = w_sb[:].bitcast(F32)
+        keep_busy(3)
         w_banks = [flip(w_words, 0, False), flip(w_words, 1, False)]
+        keep_busy(2)
         regroup(nc.scalar.copy, w_banks[0], w_pn_words[:, 0:512])
         regroup(nc.vector.tensor_copy, w_banks[1], w_pn_words[:, 512:1024])
 
         runs = cut(RUNS)
         for t in runs[0]:
             turn(t)
+            keep_busy(1)
 
         pos = w_pn[:, 0:2048].rearrange("p (q e) -> p q e", q=4)
         neg = w_pn[:, 2048:4096].rearrange("p (q e) -> p q e", q=4)
@@ -246,6 +257,8 @@ def tile_qdense_t_kernel(tc, x, W_rr, W_ri, W_rj, W_rk, b_rr, b_ri, b_rj, b_rk, 
             turns = runs[k + 1] if k + 1 < len(runs) else []
             for t in turns:
                 turn(t)
+                if k == 0:
+                    keep_busy(1)
             for t in carried:
                 finish(t)
             ahead = runs[k + 3] if k + 3 < len(runs) else []

from contextlib import ExitStack

import concourse.mybir as mybir
from concourse.masks import make_identity

F32 = mybir.dt.float32
BF16 = mybir.dt.bfloat16
U32 = mybir.dt.uint32
U8 = mybir.dt.uint8
I32 = mybir.dt.int32
FP8X4 = mybir.dt.float8_e4m3fn_x4
ADD = mybir.AluOpType.add
MULT = mybir.AluOpType.mult

P = 128
TILES = 32
FLOPS = 2 * 16384 * 512 * 512

T_BANKS = 4
M_BANKS = 4
RUNS = [2] * 16
LOADS = [(t, 1) for t in range(4)] + [(t, 2) for t in range(4, 12, 2)] + [(t, 4) for t in range(12, 32, 4)]
LOADS_AHEAD = 11
STORE_TILES = 4


def cut(runs):
    got = []
    first = 0
    for n in runs:
        got.append(list(range(first, first + n)))
        first += n
    return got


def tile_qdense_t_kernel(tc, x, W_rr, W_ri, W_rj, W_rk, b_rr, b_ri, b_rj, b_rk, out):
    nc = tc.nc
    weights = [W_rr, W_ri, W_rj, W_rk]
    biases = [b_rr, b_ri, b_rj, b_rk]
    x_rows = x.rearrange("(p t) k -> p t k", t=TILES)
    out_rows = out.rearrange("(p t) n -> p t n", t=TILES)

    with ExitStack() as ctx:
        const = ctx.enter_context(tc.tile_pool(name="const", bufs=1))
        xpool = ctx.enter_context(tc.tile_pool(name="xin", bufs=3))
        ppool = ctx.enter_context(tc.tile_pool(name="sorted", bufs=6))
        gpool = ctx.enter_context(tc.tile_pool(name="grouped", bufs=5))
        qpool = ctx.enter_context(tc.tile_pool(name="codes", bufs=10))
        opool = ctx.enter_context(tc.tile_pool(name="outs", bufs=4))
        psum = ctx.enter_context(tc.psum_pool(name="psum", bufs=1))
        ctx.enter_context(tc.manual_schedule())

        used = {"t": 0, "m": 0}

        def new_bank(kind):
            b = used[kind] % (T_BANKS if kind == "t" else M_BANKS)
            used[kind] += 1
            return psum.tile([P, 512], F32, name="%s%d" % (kind, b), tag="%s%d" % (kind, b))

        ident = const.tile([P, P], F32, name="ident")
        make_identity(nc, ident[:])
        warm = const.tile([P, 1], F32, name="warm")
        nc.vector.memset(warm[:], 0.0)
        filler = const.tile([P, 512], BF16, name="filler")
        nc.vector.memset(filler[:], 0.0)
        filler_ps = new_bank("m")

        def keep_busy(n):
            for i in range(n):
                nc.tensor.matmul(filler_ps[:], lhsT=filler[:, 0:P], rhs=filler[:], start=True, stop=True)

        b_rows = const.tile([P, P], BF16, name="b_rows")
        nc.vector.memset(b_rows[:], 0.0)
        nc.scalar.copy(out=warm[:], in_=warm[:])

        w_sb = const.tile([P, 2048], BF16, name="w_sb")
        for q in range(4):
            nc.sync.dma_start(out=w_sb[:, 512 * q:512 * (q + 1)], in_=weights[q])
        x_words = {}

        def load(i):
            t0, nt = LOADS[i]
            if t0 < 12:
                xs = const.tile([P, 2048 * nt], BF16, name="x%d" % t0)
            else:
                xs = xpool.tile([P, 2048 * nt], BF16, name="x", tag="x")
            nc.sync.dma_start(out=xs[:].rearrange("p (t k) -> p t k", t=nt),
                              in_=x_rows[:, t0:t0 + nt, :])
            words = xs[:].bitcast(F32)
            for j in range(nt):
                x_words[t0 + j] = words[:, 1024 * j:1024 * (j + 1)]

        for i in range(4):
            load(i)
        for q in range(4):
            nc.scalar.dma_start(out=b_rows[32 * q:32 * q + 1, :],
                                in_=biases[q].rearrange("(o n) -> o n", o=1))
        for i in range(4, LOADS_AHEAD):
            load(i)

        q_scales = const.tile([P, 1024], U8, name="q_scales", align_bytes=64)
        nc.vector.memset(q_scales[:].bitcast(I32), 0)
        ones = const.tile([P, P], BF16, name="ones")
        nc.vector.memset(ones[:], 1.0)
        signs = const.tile([P, 4, P], BF16, name="signs")
        nc.vector.memset(signs[:], 1.0)
        nc.vector.memset(signs[32:64, 0, :], -1.0)
        nc.vector.memset(signs[64:128, 0, :], -1.0)
        nc.vector.memset(signs[64:96, 1, :], -1.0)
        nc.vector.memset(signs[96:128, 2, :], -1.0)
        nc.vector.memset(signs[32:64, 3, :], -1.0)

        def flip(words, h, is_sorted):
            bank = new_bank("t")
            for c in range(2):
                for u in range(2):
                    base = 512 * h + 256 * c
                    if is_sorted:
                        cols = words[:, base + P * u:base + P * (u + 1)]
                    else:
                        cols = words[:, base + u:base + 256:2]
                    s = 2 * c + u
                    nc.tensor.transpose(bank[:, P * s:P * (s + 1)], cols, ident[:])
            return bank

        def regroup(engine_copy, bank, dst_words):
            engine_copy(out=dst_words.rearrange("p (c r u) -> p c r u", c=2, u=2),
                        in_=bank[:].rearrange("p (c u r) -> p c r u", c=2, u=2))

        grouped = {}
        packed = {}
        accs = {}
        done_words = {}
        outs = {}

        def put_in_order(t):
            engine_copy = nc.scalar.copy if t % 4 == 3 else nc.vector.tensor_copy
            ps = ppool.tile([P, 1024], F32, name="sorted", tag="sorted", align_bytes=64)
            engine_copy(out=ps[:].rearrange("p (c u r) -> p c u r", c=4, u=2),
                        in_=x_words[t].rearrange("p (c r u) -> p c u r", c=4, u=2))
            done_words[t] = ps[:]

        def turn(t):
            gr = gpool.tile([P, 2048], BF16, name="grouped", tag="grouped", align_bytes=64)
            gw = gr[:].bitcast(F32)
            for h in range(2):
                if t in done_words:
                    bank = flip(done_words[t], h, True)
                else:
                    bank = flip(x_words[t], h, False)
                regroup(nc.scalar.copy, bank, gw[:, 512 * h:512 * (h + 1)])
            grouped[t] = gr

        def quantise(t):
            codes = qpool.tile([P, 512], U32, name="codes", tag="codes", align_bytes=64)
            scales = qpool.tile([P, 512], U8, name="scales", tag="scales", align_bytes=64)
            nc.vector.quantize_mx(out=codes[:].bitcast(FP8X4), scales=scales[:], in_=grouped[t][:])
            packed[t] = (codes, scales)

        w_pn = const.tile([P, 4096], BF16, name="w_pn", align_bytes=64)
        w_pn_words = w_pn[:].bitcast(F32)
        w_words = w_sb[:].bitcast(F32)
        keep_busy(3)
        w_banks = [flip(w_words, 0, False), flip(w_words, 1, False)]
        keep_busy(2)
        regroup(nc.scalar.copy, w_banks[0], w_pn_words[:, 0:512])
        regroup(nc.vector.tensor_copy, w_banks[1], w_pn_words[:, 512:1024])

        runs = cut(RUNS)
        for t in runs[0]:
            turn(t)
            keep_busy(1)

        pos = w_pn[:, 0:2048].rearrange("p (q e) -> p q e", q=4)
        neg = w_pn[:, 2048:4096].rearrange("p (q e) -> p q e", q=4)
        nc.vector.tensor_scalar_mul(out=neg[:, 0:2, :], in0=pos[:, 1:4:2, :], scalar1=-1.0)
        nc.vector.tensor_scalar_mul(out=neg[:, 2:4, :], in0=pos[:, 2:4, :], scalar1=-1.0)
        q_codes = const.tile([P, 1024], U32, name="q_codes", align_bytes=64)
        nc.vector.quantize_mx(out=q_codes[:, 0:512].bitcast(FP8X4), scales=q_scales[:, 0:512],
                              in_=w_pn[:, 0:2048])
        nc.vector.quantize_mx(out=q_codes[:, 512:1024].bitcast(FP8X4), scales=q_scales[:, 512:1024],
                              in_=w_pn[:, 2048:4096])
        quantise(0)

        r_codes = const.tile([P, 1536], U32, name="r_codes", align_bytes=64)
        r_scales = const.tile([P, 1536], U8, name="r_scales", align_bytes=64)
        r_code_blocks = r_codes[:].bitcast(I32).rearrange("p (d w) -> p d w", d=12)
        q_code_blocks = q_codes[:].bitcast(I32).rearrange("p (d w) -> p d w", d=8)
        r_scale_blocks = r_scales[:].bitcast(I32).rearrange("p (d w) -> p d w", d=12)
        q_scale_blocks = q_scales[:].bitcast(I32).rearrange("p (d w) -> p d w", d=8)

        def move(dst, src, repeat=1):
            for r_blocks, q_blocks, words in [(r_code_blocks, q_code_blocks, P), (r_scale_blocks, q_scale_blocks, P // 4)]:
                blocks = q_blocks[:, src, :]
                if repeat > 1:
                    blocks = blocks.to_broadcast([P, repeat, words])
                nc.vector.tensor_copy(out=r_blocks[:, dst, :], in_=blocks)

        rhs = [(q_codes[:, 0:512], q_scales[:, 0:512])]
        for c in range(3):
            rhs.append((r_codes[:, 512 * c:512 * (c + 1)], r_scales[:, 512 * c:512 * (c + 1)]))

        move(slice(1, 12, 5), slice(0, 1), repeat=3)
        move(slice(3, 6, 2), slice(2, 4))
        move(slice(10, 11), slice(1, 2))
        move(slice(0, 5, 2), slice(4, 7))
        move(slice(7, 10), slice(4, 7))
        quantise(1)
        b_signed = const.tile([P, 4, P], BF16, name="b_signed")
        nc.vector.tensor_tensor(out=b_signed[:], in0=signs[:],
                                in1=b_rows[:].unsqueeze(1).to_broadcast([P, 4, P]), op=MULT)

        for t in runs[2]:
            put_in_order(t)
        bias_bc = const.tile([P, 512], F32, name="bias_bc")

        def spread_bias():
            bias_ps = new_bank("m")
            nc.tensor.matmul(bias_ps[:], lhsT=ones[:], rhs=b_signed[:].rearrange("p o n -> p (o n)"),
                             start=True, stop=True)
            nc.scalar.copy(out=bias_bc[:], in_=bias_ps[:])

        def multiply(t):
            codes, scales = packed[t]
            parts = 2 if t == TILES - 1 else 1
            width = 512 // parts
            accs[t] = []
            for part in range(parts):
                acc = new_bank("m")
                cols = slice(width * part, width * (part + 1))
                for c in range(4):
                    nc.tensor.matmul_mx(out=acc[:, 0:width],
                                        lhsT=codes[:, P * c:P * (c + 1)].bitcast(FP8X4),
                                        lhsT_scale=scales[:, P * c:P * (c + 1)],
                                        rhs=rhs[c][0][:, cols].bitcast(FP8X4),
                                        rhs_scale=rhs[c][1][:, cols],
                                        start=(c == 0), stop=(c == 3))
                accs[t].append((acc, width, cols))

        def finish(t):
            j = t % STORE_TILES
            if j == 0:
                outs[t // STORE_TILES] = opool.tile([P, STORE_TILES, 512], F32, name="ot", tag="ot")
            ot = outs[t // STORE_TILES]
            for acc, width, cols in accs[t]:
                nc.vector.tensor_tensor(out=ot[:, j, cols], in0=acc[:, 0:width], in1=bias_bc[:, cols], op=ADD)
                if t >= TILES - 2:
                    nc.sync.dma_start(out=out_rows[:, t, cols], in_=ot[:, j, cols])
            if t == TILES - 3:
                nc.sync.dma_start(out=out_rows[:, t - 1:t + 1, :], in_=ot[:, 0:2, :])
            elif j == STORE_TILES - 1 and t < TILES - 2:
                nc.sync.dma_start(out=out_rows[:, t - j:t + 1, :], in_=ot[:])

        n_loaded = LOADS_AHEAD
        carried = []
        for k in range(len(runs)):
            turns = runs[k + 1] if k + 1 < len(runs) else []
            for t in turns:
                turn(t)
                if k == 0:
                    keep_busy(1)
            for t in carried:
                finish(t)
            ahead = runs[k + 3] if k + 3 < len(runs) else []
            n_sorted = 0
            for n, t in enumerate(runs[k]):
                multiply(t)
                if t == runs[0][-1]:
                    spread_bias()
                if n == 0 and k >= 3:
                    for ta in ahead[0:1]:
                        put_in_order(ta)
                        n_sorted += 1
                if n < len(turns):
                    quantise(turns[n])
                if n >= 1:
                    finish(runs[k][n - 1])
                if n == len(runs[k]) - 1:
                    for tq in turns[len(runs[k]):]:
                        quantise(tq)
                    for ta in ahead[n_sorted:]:
                        put_in_order(ta)
            if n_loaded < len(LOADS) and LOADS[n_loaded][0] - 12 + 4 <= runs[k][-1] + 7:
                load(n_loaded)
                n_loaded += 1
            carried = [runs[k][-1]]
        for t in carried:
            finish(t)
